import numpy as np
import ml_dtypes


def mxq(x, axis, fmt="e4m3"):
    dtype, down = {"e4m3": (ml_dtypes.float8_e4m3fn, 7), "e5m2": (ml_dtypes.float8_e5m2, 14)}[fmt]
    v = np.moveaxis(np.asarray(x, np.float32).astype(ml_dtypes.bfloat16).astype(np.float64), axis, -1)
    blocks = v.reshape(v.shape[:-1] + (-1, 32))
    amax = np.abs(blocks).max(-1, keepdims=True)
    byte = np.maximum(np.where(amax > 0, np.frexp(amax)[1] - 1 + 127, 0) - down, 1)
    scale = np.exp2(byte - 127.0)
    codes = (blocks / scale).astype(np.float32).astype(dtype).astype(np.float64)
    return np.moveaxis((codes * scale).reshape(v.shape), -1, axis)


WIDE = False


def mx_kscale(k):
    if not WIDE:
        return np.ones(k)
    levels = np.array([10, -10, 5, -5, 0])
    a = np.random.permutation(np.resize(levels, k // 512 * 4)).reshape(k // 512, 4)
    idx = np.arange(k)
    return np.exp2(a[idx // 512, idx % 128 // 32])


BF16 = ml_dtypes.bfloat16


def bf(x):
    return np.asarray(x, np.float32).astype(BF16)


def f64(x):
    return np.asarray(x).astype(np.float64)


B, T, D, H, F = 2, 256, 1024, 8, 4096


def erf(z):
    a = np.minimum(np.abs(z), 6.0)
    y = 2.0 * a * a
    term = a.copy()
    total = a.copy()
    n = 0.0
    while np.any(term > 1e-18 * total):
        n += 1.0
        term = term * (y / (2.0 * n + 1.0))
        total = total + term
    return np.sign(z) * (2.0 / np.sqrt(np.pi)) * np.exp(-a * a) * total


def gelu_erf(v):
    return 0.5 * v * (1.0 + erf(v / np.sqrt(2.0)))


def setup_inputs():
    s = mx_kscale(D)
    return {
        "x": bf(np.random.standard_normal((B, T, D))),
        "attn_merged": bf(np.random.standard_normal((B, T, D)) * 0.6 * s),
        "w_proj": bf(np.random.standard_normal((D, D)) * 1.5 / np.sqrt(D) / s[:, None]),
        "w_ff1": bf(np.random.standard_normal((D, F)) / np.sqrt(D)),
        "b_ff1": bf(np.random.standard_normal(F) * 0.3),
        "w_ff2": bf(np.random.standard_normal((F, D)) * 1.5 / np.sqrt(F)),
        "b_ff2": bf(np.random.standard_normal(D) * 0.3),
    }


def reference(x, attn_merged, w_proj, w_ff1, b_ff1, w_ff2, b_ff2):
    x = f64(x)
    attn_out = mxq(f64(attn_merged), 2, "e4m3") @ mxq(f64(w_proj), 0, "e4m3")
    h = gelu_erf((mxq(x, 2, "e4m3") @ mxq(f64(w_ff1), 0, "e4m3")) + f64(b_ff1))
    ff_out = (mxq(h, 2, "e4m3") @ mxq(f64(w_ff2), 0, "e4m3")) + f64(b_ff2)
    return x + attn_out + ff_out

@@ -1,0 +1,263 @@
+from contextlib import ExitStack
+
+import concourse.mybir as mybir
+from concourse.masks import make_identity
+
+BF16 = mybir.dt.bfloat16
+F32 = mybir.dt.float32
+U32 = mybir.dt.uint32
+U8 = mybir.dt.uint8
+FP8X4 = mybir.dt.float8_e4m3fn_x4
+GELU = mybir.ActivationFunctionType.Gelu
+ADD = mybir.AluOpType.add
+
+P = 128
+PACK = 4
+K_PASS = P * PACK
+TOKENS = 512
+TOKEN_TILES = TOKENS // P
+D = 1024
+F = 4096
+HALF = 512
+RUN = 4
+
+D_PASSES = D // K_PASS
+FF1_STEPS = F // HALF
+PROJ_STEPS = D_PASSES
+FF2_STEPS = F // K_PASS
+STEPS = FF1_STEPS + PROJ_STEPS + FF2_STEPS
+RAW_BUFS = 8
+
+FLOPS = 2 * TOKENS * (D * D + 2 * D * F)
+
+
+def tile_block_pa_kernel(tc, x, attn_merged, w_proj, w_ff1, b_ff1, w_ff2, b_ff2, out):
+    nc = tc.nc
+    x_rows = x.flatten_outer_dims()
+    attn_rows = attn_merged.flatten_outer_dims()
+    out_rows = out.flatten_outer_dims()
+
+    with ExitStack() as stack:
+        stack.enter_context(tc.manual_schedule())
+        keep = stack.enter_context(tc.tile_pool(name="keep", bufs=1))
+        act_pool = stack.enter_context(tc.tile_pool(name="act", bufs=2))
+        raw_pool = stack.enter_context(tc.tile_pool(name="raw", bufs=RAW_BUFS))
+        grouped_pool = stack.enter_context(tc.tile_pool(name="grouped", bufs=3))
+        codes_pool = stack.enter_context(tc.tile_pool(name="codes", bufs=3))
+        h_pool = stack.enter_context(tc.tile_pool(name="h", bufs=2))
+        out_pool = stack.enter_context(tc.tile_pool(name="result", bufs=4))
+        psum = stack.enter_context(tc.psum_pool(name="psum", bufs=8))
+
+        x_sb = keep.tile([P, TOKEN_TILES, D], BF16, name="x_sb")
+        attn_sb = keep.tile([P, TOKEN_TILES, D], BF16, name="attn_sb")
+        for i in range(TOKEN_TILES):
+            nc.sync.dma_start(out=x_sb[:, i, :], in_=x_rows[i * P : (i + 1) * P, :])
+        for i in range(TOKEN_TILES):
+            nc.sync.dma_start(out=attn_sb[:, i, :], in_=attn_rows[i * P : (i + 1) * P, :])
+
+        b1_rows = keep.tile([P, P], BF16, name="b1_rows")
+        nc.vector.memset(b1_rows[:], 0.0)
+        nc.scalar.dma_start(out=b1_rows[0 : F // P, :], in_=b_ff1.rearrange("(r c) -> r c", c=P))
+        b2_all = keep.tile([P, D], BF16, name="b2_all")
+        nc.scalar.dma_start(out=b2_all[:], in_=b_ff2.partition_broadcast(P))
+
+        warm = keep.tile([P, 1], F32, name="warm")
+        nc.vector.memset(warm[:], 0.0)
+        nc.scalar.activation(out=warm[:], in_=warm[:], func=GELU)
+
+        ident_f32 = keep.tile([P, P], F32, name="ident_f32")
+        make_identity(nc, ident_f32[:])
+        ident_bf16 = keep.tile([P, P], BF16, name="ident_bf16")
+        make_identity(nc, ident_bf16[:])
+
+        def load_weight_tile(step):
+            raw = raw_pool.tile([P, 2 * PACK * HALF], BF16, name="raw")
+            if step < FF1_STEPS:
+                halves = raw[:].rearrange("p (g t c) -> p g t c", g=2, t=PACK)
+                cols = slice(step * HALF, (step + 1) * HALF)
+                for g in range(D_PASSES):
+                    for u in range(2):
+                        first = g * K_PASS + u * 2 * P
+                        nc.sync.dma_start(
+                            out=halves[:, g, 2 * u : 2 * u + 2, :],
+                            in_=w_ff1[first : first + 2 * P, cols].rearrange("(q e) c -> q e c", e=2),
+                        )
+                return [halves[:, 0, :, :], halves[:, 1, :, :]]
+            rows = raw[:].rearrange("p (t n) -> p t n", t=PACK)
+            if step < FF1_STEPS + PROJ_STEPS:
+                g = step - FF1_STEPS
+                for u in range(2):
+                    first = g * K_PASS + u * 2 * P
+                    nc.sync.dma_start(
+                        out=rows[:, 2 * u : 2 * u + 2, :],
+                        in_=w_proj[first : first + 2 * P, :].rearrange("(q e) n -> q e n", e=2),
+                    )
+            else:
+                g = step - FF1_STEPS - PROJ_STEPS
+                nc.sync.dma_start(
+                    out=rows,
+                    in_=w_ff2[g * K_PASS : (g + 1) * K_PASS, :].rearrange("(t p) n -> p t n", p=P),
+                )
+            return [rows[:, :, 0:HALF], rows[:, :, HALF : 2 * HALF]]
+
+        def regroup(copy, grouped, rows):
+            copy(
+                out=grouped[:].rearrange("p (c i) t -> p c t i", i=RUN),
+                in_=rows.rearrange("p t (c i) -> p c t i", i=RUN),
+            )
+
+        def quantise(grouped, codes, scales):
+            nc.vector.quantize_mx(
+                out=codes.bitcast(FP8X4),
+                scales=scales,
+                in_=grouped[:].rearrange("p c t -> p (c t)"),
+            )
+
+        raw_halves = {}
+        for step in range(RAW_BUFS):
+            raw_halves[step] = load_weight_tile(step)
+
+        def x_words(rows_sb, i):
+            return rows_sb[:, i, :].bitcast(F32)
+
+        def transpose_and_quantise(rows_sb, codes, scales):
+            grouped = act_pool.tile([P, D_PASSES, TOKENS * PACK], BF16, name="act_grouped", align_bytes=64)
+            for g in range(D_PASSES):
+                grouped_words = grouped[:, g, :].bitcast(F32)
+                for pair in range(TOKEN_TILES // 2):
+                    bank = psum.tile([P, 2, 2 * P], F32, name="bank")
+                    for u in range(2):
+                        for j in range(2):
+                            words = x_words(rows_sb, 2 * pair + j)
+                            first = g * 2 * P + u * P
+                            nc.tensor.transpose(
+                                out=bank[:, u, j * P : (j + 1) * P],
+                                in_=words[:, first : first + P],
+                                identity=ident_f32[:],
+                            )
+                    nc.scalar.copy(
+                        out=grouped_words[:, pair * 4 * P : (pair + 1) * 4 * P].rearrange("p (r u) -> p r u", u=2),
+                        in_=bank[:].rearrange("p u r -> p r u"),
+                    )
+            for g in range(D_PASSES):
+                nc.vector.quantize_mx(
+                    out=codes[:, g, :].bitcast(FP8X4), scales=scales[:, g, :], in_=grouped[:, g, :]
+                )
+
+        x_codes = keep.tile([P, D_PASSES, TOKENS], U32, name="x_codes", align_bytes=64)
+        x_scales = keep.tile([P, D_PASSES, TOKENS], U8, name="x_scales", align_bytes=64)
+        attn_codes = keep.tile([P, D_PASSES, TOKENS], U32, name="attn_codes", align_bytes=64)
+        attn_scales = keep.tile([P, D_PASSES, TOKENS], U8, name="attn_scales", align_bytes=64)
+
+        x_plus_b2 = keep.tile([P, TOKEN_TILES, D], F32, name="x_plus_b2")
+        for i in range(TOKEN_TILES):
+            nc.vector.tensor_tensor(out=x_plus_b2[:, i, :], in0=x_sb[:, i, :], in1=b2_all[:], op=ADD)
+
+        transpose_and_quantise(x_sb, x_codes, x_scales)
+
+        b1_bank = psum.tile([P, P], BF16, name="bank")
+        nc.tensor.transpose(out=b1_bank[:], in_=b1_rows[:], identity=ident_bf16[:])
+        b1 = keep.tile([P, F // P], F32, name="b1")
+        nc.vector.tensor_copy(out=b1[:], in_=b1_bank[:, 0 : F // P])
+
+        transpose_and_quantise(attn_sb, attn_codes, attn_scales)
+
+        h_codes = keep.tile([P, FF2_STEPS, TOKENS], U32, name="h_codes", align_bytes=64)
+        h_scales = keep.tile([P, FF2_STEPS, TOKENS], U8, name="h_scales", align_bytes=64)
+        grouped_halves = {}
+        hidden_banks = {}
+        h_rows = {}
+        h_grouped = {}
+        acc = {}
+
+        def regroup_weights(step):
+            first = grouped_pool.tile([P, HALF, PACK], BF16, name="grouped_first", align_bytes=64)
+            second = grouped_pool.tile([P, HALF, PACK], BF16, name="grouped_second", align_bytes=64)
+            regroup(nc.vector.tensor_copy, first, raw_halves[step][0])
+            regroup(nc.scalar.copy, second, raw_halves[step][1])
+            grouped_halves[step] = [first, second]
+
+        def quantise_weights(step):
+            operands = []
+            for half in range(2):
+                codes = codes_pool.tile([P, HALF], U32, name="codes%d" % half, align_bytes=64)
+                scales = codes_pool.tile([P, HALF], U8, name="scales%d" % half, align_bytes=64)
+                quantise(grouped_halves[step][half], codes[:], scales[:])
+                operands.append((codes, scales))
+            return operands
+
+        def multiply_ff1(step, operands):
+            hidden_banks[step] = []
+            for t in range(PACK):
+                bank = psum.tile([P, TOKENS], F32, name="bank")
+                for g in range(D_PASSES):
+                    codes, scales = operands[g]
+                    nc.tensor.matmul_mx(
+                        out=bank[:],
+                        lhsT=codes[:, t * P : (t + 1) * P].bitcast(FP8X4),
+                        lhsT_scale=scales[:, t * P : (t + 1) * P],
+                        rhs=x_codes[:, g, :].bitcast(FP8X4),
+                        rhs_scale=x_scales[:, g, :],
+                        start=(g == 0),
+                        stop=(g == D_PASSES - 1),
+                    )
+                hidden_banks[step].append(bank)
+
+        def multiply_into_result(step, operands):
+            if step < FF1_STEPS + PROJ_STEPS:
+                g = step - FF1_STEPS
+                left_codes, left_scales = attn_codes, attn_scales
+            else:
+                g = step - FF1_STEPS - PROJ_STEPS
+                left_codes, left_scales = h_codes, h_scales
+            for half in range(2):
+                codes, scales = operands[half]
+                for i in range(TOKEN_TILES):
+                    if step == FF1_STEPS:
+                        acc[(i, half)] = psum.tile([P, HALF], F32, name="bank")
+                    nc.tensor.matmul_mx(
+                        out=acc[(i, half)][:],
+                        lhsT=left_codes[:, g, i * P : (i + 1) * P].bitcast(FP8X4),
+                        lhsT_scale=left_scales[:, g, i * P : (i + 1) * P],
+                        rhs=codes[:].bitcast(FP8X4),
+                        rhs_scale=scales[:],
+                        start=(step == FF1_STEPS),
+                        stop=(step == STEPS - 1),
+                    )
+
+        def gelu(step):
+            h_rows[step] = h_pool.tile([P, PACK, TOKENS], BF16, name="h_rows")
+            for t in range(PACK):
+                j = step * PACK + t
+                nc.scalar.activation(
+                    out=h_rows[step][:, t, :], in_=hidden_banks[step][t][:], func=GELU, bias=b1[:, j : j + 1]
+                )
+
+        def regroup_h(step):
+            h_grouped[step] = h_pool.tile([P, TOKENS, PACK], BF16, name="h_grouped", align_bytes=64)
+            regroup(nc.vector.tensor_copy, h_grouped[step], h_rows[step][:])
+
+        for now in range(STEPS + 1):
+            if 0 <= now - 2 < FF1_STEPS:
+                gelu(now - 2)
+            if now < STEPS:
+                regroup_weights(now)
+            if 0 <= now - 4 < FF1_STEPS:
+                quantise(h_grouped[now - 4], h_codes[:, now - 4, :], h_scales[:, now - 4, :])
+            if 0 <= now - 1:
+                operands = quantise_weights(now - 1)
+                if now - 1 < FF1_STEPS:
+                    multiply_ff1(now - 1, operands)
+                else:
+                    multiply_into_result(now - 1, operands)
+            if 0 <= now - 3 < FF1_STEPS:
+                regroup_h(now - 3)
+            if now + RAW_BUFS < STEPS:
+                raw_halves[now + RAW_BUFS] = load_weight_tile(now + RAW_BUFS)
+
+        for half in range(2):
+            cols = slice(half * HALF, (half + 1) * HALF)
+            for i in range(TOKEN_TILES):
+                result = out_pool.tile([P, HALF], F32, name="result")
+                nc.vector.tensor_tensor(out=result[:], in0=acc[(i, half)][:], in1=x_plus_b2[:, i, cols], op=ADD)
+                nc.sync.dma_start(out=out_rows[i * P : (i + 1) * P, cols], in_=result[:])

@@ -19,6 +19,7 @@ TOKEN_TILES = TOKENS // P
 D = 1024
 F = 4096
 HALF = 512
+TILE_COLS = 2 * HALF
 RUN = 4
 
 D_PASSES = D // K_PASS
@@ -27,6 +28,9 @@ PROJ_STEPS = D_PASSES
 FF2_STEPS = F // K_PASS
 STEPS = FF1_STEPS + PROJ_STEPS + FF2_STEPS
 RAW_BUFS = 8
+VECTOR_COLS_BESIDE_GELU = 640
+VECTOR_COLS_ALONE = 448
+ATTN_ROUND = 6
 
 FLOPS = 2 * TOKENS * (D * D + 2 * D * F)
 
@@ -52,14 +56,15 @@ def tile_block_pa_kernel(tc, x, attn_merged, w_proj, w_ff1, b_ff1, w_ff2, b_ff2,
         attn_sb = keep.tile([P, TOKEN_TILES, D], BF16, name="attn_sb")
         for i in range(TOKEN_TILES):
             nc.sync.dma_start(out=x_sb[:, i, :], in_=x_rows[i * P : (i + 1) * P, :])
-        for i in range(TOKEN_TILES):
-            nc.sync.dma_start(out=attn_sb[:, i, :], in_=attn_rows[i * P : (i + 1) * P, :])
 
+        b2_row = keep.tile([P, D], BF16, name="b2_row")
+        nc.vector.memset(b2_row[:], 0.0)
+        nc.scalar.dma_start(out=b2_row[0:1, :], in_=b_ff2.rearrange("(o d) -> o d", o=1))
+        ones = keep.tile([P, P], BF16, name="ones")
+        nc.vector.memset(ones[:], 1.0)
         b1_rows = keep.tile([P, P], BF16, name="b1_rows")
         nc.vector.memset(b1_rows[:], 0.0)
         nc.scalar.dma_start(out=b1_rows[0 : F // P, :], in_=b_ff1.rearrange("(r c) -> r c", c=P))
-        b2_all = keep.tile([P, D], BF16, name="b2_all")
-        nc.scalar.dma_start(out=b2_all[:], in_=b_ff2.partition_broadcast(P))
 
         warm = keep.tile([P, 1], F32, name="warm")
         nc.vector.memset(warm[:], 0.0)
@@ -71,38 +76,35 @@ def tile_block_pa_kernel(tc, x, attn_merged, w_proj, w_ff1, b_ff1, w_ff2, b_ff2,
         make_identity(nc, ident_bf16[:])
 
         def load_weight_tile(step):
-            raw = raw_pool.tile([P, 2 * PACK * HALF], BF16, name="raw")
+            raw = raw_pool.tile([P, PACK, TILE_COLS], BF16, name="raw")
             if step < FF1_STEPS:
-                halves = raw[:].rearrange("p (g t c) -> p g t c", g=2, t=PACK)
                 cols = slice(step * HALF, (step + 1) * HALF)
                 for g in range(D_PASSES):
                     for u in range(2):
                         first = g * K_PASS + u * 2 * P
                         nc.sync.dma_start(
-                            out=halves[:, g, 2 * u : 2 * u + 2, :],
+                            out=raw[:, 2 * u : 2 * u + 2, g * HALF : (g + 1) * HALF],
                             in_=w_ff1[first : first + 2 * P, cols].rearrange("(q e) c -> q e c", e=2),
                         )
-                return [halves[:, 0, :, :], halves[:, 1, :, :]]
-            rows = raw[:].rearrange("p (t n) -> p t n", t=PACK)
-            if step < FF1_STEPS + PROJ_STEPS:
+            elif step < FF1_STEPS + PROJ_STEPS:
                 g = step - FF1_STEPS
                 for u in range(2):
                     first = g * K_PASS + u * 2 * P
                     nc.sync.dma_start(
-                        out=rows[:, 2 * u : 2 * u + 2, :],
+                        out=raw[:, 2 * u : 2 * u + 2, :],
                         in_=w_proj[first : first + 2 * P, :].rearrange("(q e) n -> q e n", e=2),
                     )
             else:
                 g = step - FF1_STEPS - PROJ_STEPS
                 nc.sync.dma_start(
-                    out=rows,
+                    out=raw[:],
                     in_=w_ff2[g * K_PASS : (g + 1) * K_PASS, :].rearrange("(t p) n -> p t n", p=P),
                 )
-            return [rows[:, :, 0:HALF], rows[:, :, HALF : 2 * HALF]]
+            return raw
 
         def regroup(copy, grouped, rows):
             copy(
-                out=grouped[:].rearrange("p (c i) t -> p c t i", i=RUN),
+                out=grouped.rearrange("p (c i) t -> p c t i", i=RUN),
                 in_=rows.rearrange("p t (c i) -> p c t i", i=RUN),
             )
 
@@ -110,17 +112,20 @@ def tile_block_pa_kernel(tc, x, attn_merged, w_proj, w_ff1, b_ff1, w_ff2, b_ff2,
             nc.vector.quantize_mx(
                 out=codes.bitcast(FP8X4),
                 scales=scales,
-                in_=grouped[:].rearrange("p c t -> p (c t)"),
+                in_=grouped.rearrange("p c t -> p (c t)"),
             )
 
-        raw_halves = {}
+        raw_tiles = {}
         for step in range(RAW_BUFS):
-            raw_halves[step] = load_weight_tile(step)
+            if step == ATTN_ROUND - 1:
+                for i in range(TOKEN_TILES):
+                    nc.sync.dma_start(out=attn_sb[:, i, :], in_=attn_rows[i * P : (i + 1) * P, :])
+            raw_tiles[step] = load_weight_tile(step)
 
         def x_words(rows_sb, i):
             return rows_sb[:, i, :].bitcast(F32)
 
-        def transpose_and_quantise(rows_sb, codes, scales):
+        def transpose_rows(rows_sb):
             grouped = act_pool.tile([P, D_PASSES, TOKENS * PACK], BF16, name="act_grouped", align_bytes=64)
             for g in range(D_PASSES):
                 grouped_words = grouped[:, g, :].bitcast(F32)
@@ -139,6 +144,9 @@ def tile_block_pa_kernel(tc, x, attn_merged, w_proj, w_ff1, b_ff1, w_ff2, b_ff2,
                         out=grouped_words[:, pair * 4 * P : (pair + 1) * 4 * P].rearrange("p (r u) -> p r u", u=2),
                         in_=bank[:].rearrange("p u r -> p r u"),
                     )
+            return grouped
+
+        def quantise_rows(grouped, codes, scales):
             for g in range(D_PASSES):
                 nc.vector.quantize_mx(
                     out=codes[:, g, :].bitcast(FP8X4), scales=scales[:, g, :], in_=grouped[:, g, :]
@@ -150,39 +158,47 @@ def tile_block_pa_kernel(tc, x, attn_merged, w_proj, w_ff1, b_ff1, w_ff2, b_ff2,
         attn_scales = keep.tile([P, D_PASSES, TOKENS], U8, name="attn_scales", align_bytes=64)
 
         x_plus_b2 = keep.tile([P, TOKEN_TILES, D], F32, name="x_plus_b2")
+        b2_banks = []
+        for half in range(2):
+            b2_bank = psum.tile([P, HALF], F32, name="bank")
+            nc.tensor.matmul(
+                out=b2_bank[:], lhsT=ones[:], rhs=b2_row[:, half * HALF : (half + 1) * HALF], start=True, stop=True
+            )
+            b2_banks.append(b2_bank)
         for i in range(TOKEN_TILES):
-            nc.vector.tensor_tensor(out=x_plus_b2[:, i, :], in0=x_sb[:, i, :], in1=b2_all[:], op=ADD)
+            for half in range(2):
+                cols = slice(half * HALF, (half + 1) * HALF)
+                nc.vector.tensor_tensor(out=x_plus_b2[:, i, cols], in0=b2_banks[half][:], in1=x_sb[:, i, cols], op=ADD)
 
-        transpose_and_quantise(x_sb, x_codes, x_scales)
+        quantise_rows(transpose_rows(x_sb), x_codes, x_scales)
 
         b1_bank = psum.tile([P, P], BF16, name="bank")
         nc.tensor.transpose(out=b1_bank[:], in_=b1_rows[:], identity=ident_bf16[:])
         b1 = keep.tile([P, F // P], F32, name="b1")
         nc.vector.tensor_copy(out=b1[:], in_=b1_bank[:, 0 : F // P])
 
-        transpose_and_quantise(attn_sb, attn_codes, attn_scales)
-
         h_codes = keep.tile([P, FF2_STEPS, TOKENS], U32, name="h_codes", align_bytes=64)
         h_scales = keep.tile([P, FF2_STEPS, TOKENS], U8, name="h_scales", align_bytes=64)
-        grouped_halves = {}
+        grouped_tiles = {}
+        attn_grouped = {}
         hidden_banks = {}
         h_rows = {}
         h_grouped = {}
         acc = {}
 
-        def regroup_weights(step):
-            first = grouped_pool.tile([P, HALF, PACK], BF16, name="grouped_first", align_bytes=64)
-            second = grouped_pool.tile([P, HALF, PACK], BF16, name="grouped_second", align_bytes=64)
-            regroup(nc.vector.tensor_copy, first, raw_halves[step][0])
-            regroup(nc.scalar.copy, second, raw_halves[step][1])
-            grouped_halves[step] = [first, second]
+        def regroup_weights(step, vector_cols):
+            grouped = grouped_pool.tile([P, TILE_COLS, PACK], BF16, name="grouped", align_bytes=64)
+            raw = raw_tiles[step]
+            regroup(nc.vector.tensor_copy, grouped[:, 0:vector_cols, :], raw[:, :, 0:vector_cols])
+            regroup(nc.scalar.copy, grouped[:, vector_cols:TILE_COLS, :], raw[:, :, vector_cols:TILE_COLS])
+            grouped_tiles[step] = grouped
 
         def quantise_weights(step):
             operands = []
             for half in range(2):
                 codes = codes_pool.tile([P, HALF], U32, name="codes%d" % half, align_bytes=64)
                 scales = codes_pool.tile([P, HALF], U8, name="scales%d" % half, align_bytes=64)
-                quantise(grouped_halves[step][half], codes[:], scales[:])
+                quantise(grouped_tiles[step][:, half * HALF : (half + 1) * HALF, :], codes[:], scales[:])
                 operands.append((codes, scales))
             return operands
 
@@ -235,15 +251,20 @@ def tile_block_pa_kernel(tc, x, attn_merged, w_proj, w_ff1, b_ff1, w_ff2, b_ff2,
 
         def regroup_h(step):
             h_grouped[step] = h_pool.tile([P, TOKENS, PACK], BF16, name="h_grouped", align_bytes=64)
-            regroup(nc.vector.tensor_copy, h_grouped[step], h_rows[step][:])
+            regroup(nc.vector.tensor_copy, h_grouped[step][:], h_rows[step][:])
 
         for now in range(STEPS + 1):
-            if 0 <= now - 2 < FF1_STEPS:
+            if now == ATTN_ROUND:
+                attn_grouped[0] = transpose_rows(attn_sb)
+            scalar_has_gelu = 0 <= now - 2 < FF1_STEPS
+            if scalar_has_gelu:
                 gelu(now - 2)
             if now < STEPS:
-                regroup_weights(now)
+                regroup_weights(now, VECTOR_COLS_BESIDE_GELU if scalar_has_gelu else VECTOR_COLS_ALONE)
+            if now == ATTN_ROUND + 1:
+                quantise_rows(attn_grouped[0], attn_codes, attn_scales)
             if 0 <= now - 4 < FF1_STEPS:
-                quantise(h_grouped[now - 4], h_codes[:, now - 4, :], h_scales[:, now - 4, :])
+                quantise(h_grouped[now - 4][:], h_codes[:, now - 4, :], h_scales[:, now - 4, :])
             if 0 <= now - 1:
                 operands = quantise_weights(now - 1)
                 if now - 1 < FF1_STEPS:
@@ -253,7 +274,7 @@ def tile_block_pa_kernel(tc, x, attn_merged, w_proj, w_ff1, b_ff1, w_ff2, b_ff2,
             if 0 <= now - 3 < FF1_STEPS:
                 regroup_h(now - 3)
             if now + RAW_BUFS < STEPS:
-                raw_halves[now + RAW_BUFS] = load_weight_tile(now + RAW_BUFS)
+                raw_tiles[now + RAW_BUFS] = load_weight_tile(now + RAW_BUFS)
 
         for half in range(2):
             cols = slice(half * HALF, (half + 1) * HALF)

@@ -54,12 +54,11 @@ def tile_block_pa_kernel(tc, x, attn_merged, w_proj, w_ff1, b_ff1, w_ff2, b_ff2,
 
         x_sb = keep.tile([P, TOKEN_TILES, D], BF16, name="x_sb")
         attn_sb = keep.tile([P, TOKEN_TILES, D], BF16, name="attn_sb")
+        b2_row = keep.tile([P, D], BF16, name="b2_row")
+        nc.gpsimd.memset(b2_row[:].bitcast(F32), 0.0)
+        nc.sync.dma_start(out=b2_row[0:1, :], in_=b_ff2.rearrange("(o d) -> o d", o=1))
         for i in range(TOKEN_TILES):
             nc.sync.dma_start(out=x_sb[:, i, :], in_=x_rows[i * P : (i + 1) * P, :])
-
-        b2_row = keep.tile([P, D], BF16, name="b2_row")
-        nc.vector.memset(b2_row[:], 0.0)
-        nc.scalar.dma_start(out=b2_row[0:1, :], in_=b_ff2.rearrange("(o d) -> o d", o=1))
         ones = keep.tile([P, P], BF16, name="ones")
         nc.vector.memset(ones[:], 1.0)
         b1_rows = keep.tile([P, P], BF16, name="b1_rows")

@@ -264,14 +264,14 @@ def tile_block_pa_kernel(tc, x, attn_merged, w_proj, w_ff1, b_ff1, w_ff2, b_ff2,
                 quantise_rows(attn_grouped[0], attn_codes, attn_scales)
             if 0 <= now - 4 < FF1_STEPS:
                 quantise(h_grouped[now - 4][:], h_codes[:, now - 4, :], h_scales[:, now - 4, :])
+            if 0 <= now - 3 < FF1_STEPS:
+                regroup_h(now - 3)
             if 0 <= now - 1:
                 operands = quantise_weights(now - 1)
                 if now - 1 < FF1_STEPS:
                     multiply_ff1(now - 1, operands)
                 else:
                     multiply_into_result(now - 1, operands)
-            if 0 <= now - 3 < FF1_STEPS:
-                regroup_h(now - 3)
             if now + RAW_BUFS < STEPS:
                 raw_tiles[now + RAW_BUFS] = load_weight_tile(now + RAW_BUFS)
 

@@ -20,17 +20,22 @@ D = 1024
 F = 4096
 HALF = 512
 TILE_COLS = 2 * HALF
-RUN = 4
+RUN = 8
 
 D_PASSES = D // K_PASS
 FF1_STEPS = F // HALF
-PROJ_STEPS = D_PASSES
-FF2_STEPS = F // K_PASS
-STEPS = FF1_STEPS + PROJ_STEPS + FF2_STEPS
+H_PASSES = F // K_PASS
+TILE_PASSES = TILE_COLS // HALF
+HALF_STEPS = 1 + H_PASSES // TILE_PASSES
+HALVES = D // HALF
+STEPS = FF1_STEPS + HALVES * HALF_STEPS
 RAW_BUFS = 8
-VECTOR_COLS_BESIDE_GELU = 640
-VECTOR_COLS_ALONE = 448
-ATTN_ROUND = 6
+VECTOR_COLS_FIRST = 384
+VECTOR_COLS_BESIDE_GELU = 576
+VECTOR_COLS_ALONE = 480
+VECTOR_COLS_LAST = 192
+ATTN_LOAD = 1
+ATTN_ROUND = 1
 
 FLOPS = 2 * TOKENS * (D * D + 2 * D * F)
 
@@ -85,20 +90,24 @@ def tile_block_pa_kernel(tc, x, attn_merged, w_proj, w_ff1, b_ff1, w_ff2, b_ff2,
                             out=raw[:, 2 * u : 2 * u + 2, g * HALF : (g + 1) * HALF],
                             in_=w_ff1[first : first + 2 * P, cols].rearrange("(q e) c -> q e c", e=2),
                         )
-            elif step < FF1_STEPS + PROJ_STEPS:
-                g = step - FF1_STEPS
-                for u in range(2):
-                    first = g * K_PASS + u * 2 * P
-                    nc.sync.dma_start(
-                        out=raw[:, 2 * u : 2 * u + 2, :],
-                        in_=w_proj[first : first + 2 * P, :].rearrange("(q e) n -> q e n", e=2),
-                    )
             else:
-                g = step - FF1_STEPS - PROJ_STEPS
-                nc.sync.dma_start(
-                    out=raw[:],
-                    in_=w_ff2[g * K_PASS : (g + 1) * K_PASS, :].rearrange("(t p) n -> p t n", p=P),
-                )
+                half, tile_of_half = divmod(step - FF1_STEPS, HALF_STEPS)
+                cols = slice(half * HALF, (half + 1) * HALF)
+                for g in range(TILE_PASSES):
+                    to_cols = slice(g * HALF, (g + 1) * HALF)
+                    if tile_of_half == 0:
+                        for u in range(2):
+                            first = g * K_PASS + u * 2 * P
+                            nc.sync.dma_start(
+                                out=raw[:, 2 * u : 2 * u + 2, to_cols],
+                                in_=w_proj[first : first + 2 * P, cols].rearrange("(q e) n -> q e n", e=2),
+                            )
+                    else:
+                        first = ((tile_of_half - 1) * TILE_PASSES + g) * K_PASS
+                        nc.sync.dma_start(
+                            out=raw[:, :, to_cols],
+                            in_=w_ff2[first : first + K_PASS, cols].rearrange("(t p) n -> p t n", p=P),
+                        )
             return raw
 
         def regroup(copy, grouped, rows):
@@ -116,7 +125,7 @@ def tile_block_pa_kernel(tc, x, attn_merged, w_proj, w_ff1, b_ff1, w_ff2, b_ff2,
 
         raw_tiles = {}
         for step in range(RAW_BUFS):
-            if step == ATTN_ROUND - 1:
+            if step == ATTN_LOAD:
                 for i in range(TOKEN_TILES):
                     nc.sync.dma_start(out=attn_sb[:, i, :], in_=attn_rows[i * P : (i + 1) * P, :])
             raw_tiles[step] = load_weight_tile(step)
@@ -176,8 +185,8 @@ def tile_block_pa_kernel(tc, x, attn_merged, w_proj, w_ff1, b_ff1, w_ff2, b_ff2,
         b1 = keep.tile([P, F // P], F32, name="b1")
         nc.vector.tensor_copy(out=b1[:], in_=b1_bank[:, 0 : F // P])
 
-        h_codes = keep.tile([P, FF2_STEPS, TOKENS], U32, name="h_codes", align_bytes=64)
-        h_scales = keep.tile([P, FF2_STEPS, TOKENS], U8, name="h_scales", align_bytes=64)
+        h_codes = keep.tile([P, H_PASSES, TOKENS], U32, name="h_codes", align_bytes=64)
+        h_scales = keep.tile([P, H_PASSES, TOKENS], U8, name="h_scales", align_bytes=64)
         grouped_tiles = {}
         attn_grouped = {}
         hidden_banks = {}
@@ -219,26 +228,32 @@ def tile_block_pa_kernel(tc, x, attn_merged, w_proj, w_ff1, b_ff1, w_ff2, b_ff2,
                 hidden_banks[step].append(bank)
 
         def multiply_into_result(step, operands):
-            if step < FF1_STEPS + PROJ_STEPS:
-                g = step - FF1_STEPS
-                left_codes, left_scales = attn_codes, attn_scales
-            else:
-                g = step - FF1_STEPS - PROJ_STEPS
-                left_codes, left_scales = h_codes, h_scales
-            for half in range(2):
-                codes, scales = operands[half]
+            half, tile_of_half = divmod(step - FF1_STEPS, HALF_STEPS)
+            for g in range(TILE_PASSES):
+                codes, scales = operands[g]
+                if tile_of_half == 0:
+                    k_pass, left_codes, left_scales = g, attn_codes, attn_scales
+                else:
+                    k_pass, left_codes, left_scales = (tile_of_half - 1) * TILE_PASSES + g, h_codes, h_scales
+                opens = tile_of_half == 0 and g == 0
                 for i in range(TOKEN_TILES):
-                    if step == FF1_STEPS:
-                        acc[(i, half)] = psum.tile([P, HALF], F32, name="bank")
+                    if opens:
+                        acc[(half, i)] = psum.tile([P, HALF], F32, name="bank")
                     nc.tensor.matmul_mx(
-                        out=acc[(i, half)][:],
-                        lhsT=left_codes[:, g, i * P : (i + 1) * P].bitcast(FP8X4),
-                        lhsT_scale=left_scales[:, g, i * P : (i + 1) * P],
+                        out=acc[(half, i)][:],
+                        lhsT=left_codes[:, k_pass, i * P : (i + 1) * P].bitcast(FP8X4),
+                        lhsT_scale=left_scales[:, k_pass, i * P : (i + 1) * P],
                         rhs=codes[:].bitcast(FP8X4),
                         rhs_scale=scales[:],
-                        start=(step == FF1_STEPS),
-                        stop=(step == STEPS - 1),
+                        start=opens,
+                        stop=(tile_of_half == HALF_STEPS - 1 and g == TILE_PASSES - 1),
                     )
+
+        def finish(half, i):
+            cols = slice(half * HALF, (half + 1) * HALF)
+            result = out_pool.tile([P, HALF], F32, name="result")
+            nc.vector.tensor_tensor(out=result[:], in0=acc[(half, i)][:], in1=x_plus_b2[:, i, cols], op=ADD)
+            nc.sync.dma_start(out=out_rows[i * P : (i + 1) * P, cols], in_=result[:])
 
         def gelu(step):
             h_rows[step] = h_pool.tile([P, PACK, TOKENS], BF16, name="h_rows")
@@ -252,21 +267,33 @@ def tile_block_pa_kernel(tc, x, attn_merged, w_proj, w_ff1, b_ff1, w_ff2, b_ff2,
             h_grouped[step] = h_pool.tile([P, TOKENS, PACK], BF16, name="h_grouped", align_bytes=64)
             regroup(nc.vector.tensor_copy, h_grouped[step][:], h_rows[step][:])
 
+        def vector_cols(step):
+            if step == 0:
+                return VECTOR_COLS_FIRST
+            if step == STEPS - 1:
+                return VECTOR_COLS_LAST
+            return VECTOR_COLS_BESIDE_GELU if 0 <= step - 2 < FF1_STEPS else VECTOR_COLS_ALONE
+
         for now in range(STEPS + 1):
             if now == ATTN_ROUND:
                 attn_grouped[0] = transpose_rows(attn_sb)
             scalar_has_gelu = 0 <= now - 2 < FF1_STEPS
             if scalar_has_gelu:
                 gelu(now - 2)
+            if now == STEPS - 1:
+                multiply_into_result(now - 1, quantise_weights(now - 1))
             if now < STEPS:
-                regroup_weights(now, VECTOR_COLS_BESIDE_GELU if scalar_has_gelu else VECTOR_COLS_ALONE)
+                regroup_weights(now, vector_cols(now))
+            if now == STEPS - 1:
+                for i in range(TOKEN_TILES - 1):
+                    finish(0, i)
             if now == ATTN_ROUND + 1:
                 quantise_rows(attn_grouped[0], attn_codes, attn_scales)
             if 0 <= now - 4 < FF1_STEPS:
                 quantise(h_grouped[now - 4][:], h_codes[:, now - 4, :], h_scales[:, now - 4, :])
             if 0 <= now - 3 < FF1_STEPS:
                 regroup_h(now - 3)
-            if 0 <= now - 1:
+            if 0 <= now - 1 and now != STEPS - 1:
                 operands = quantise_weights(now - 1)
                 if now - 1 < FF1_STEPS:
                     multiply_ff1(now - 1, operands)
@@ -275,9 +302,6 @@ def tile_block_pa_kernel(tc, x, attn_merged, w_proj, w_ff1, b_ff1, w_ff2, b_ff2,
             if now + RAW_BUFS < STEPS:
                 raw_tiles[now + RAW_BUFS] = load_weight_tile(now + RAW_BUFS)
 
-        for half in range(2):
-            cols = slice(half * HALF, (half + 1) * HALF)
-            for i in range(TOKEN_TILES):
-                result = out_pool.tile([P, HALF], F32, name="result")
-                nc.vector.tensor_tensor(out=result[:], in0=acc[(i, half)][:], in1=x_plus_b2[:, i, cols], op=ADD)
-                nc.sync.dma_start(out=out_rows[i * P : (i + 1) * P, cols], in_=result[:])
+        finish(0, TOKEN_TILES - 1)
+        for i in range(TOKEN_TILES):
+            finish(HALVES - 1, i)

@@ -30,10 +30,12 @@ HALF_STEPS = 1 + H_PASSES // TILE_PASSES
 HALVES = D // HALF
 STEPS = FF1_STEPS + HALVES * HALF_STEPS
 RAW_BUFS = 8
-VECTOR_COLS_FIRST = 384
-VECTOR_COLS_BESIDE_GELU = 576
+VECTOR_COLS_FIRST = 512
+VECTOR_COLS_BESIDE_GELU = 512
 VECTOR_COLS_ALONE = 480
 VECTOR_COLS_LAST = 192
+TENSOR_COLS = 256
+UNIT = HALF // PACK
 ATTN_LOAD = 1
 ATTN_ROUND = 1
 
@@ -188,6 +190,7 @@ def tile_block_pa_kernel(tc, x, attn_merged, w_proj, w_ff1, b_ff1, w_ff2, b_ff2,
         h_codes = keep.tile([P, H_PASSES, TOKENS], U32, name="h_codes", align_bytes=64)
         h_scales = keep.tile([P, H_PASSES, TOKENS], U8, name="h_scales", align_bytes=64)
         grouped_tiles = {}
+        staged_banks = {}
         attn_grouped = {}
         hidden_banks = {}
         h_rows = {}
@@ -198,8 +201,30 @@ def tile_block_pa_kernel(tc, x, attn_merged, w_proj, w_ff1, b_ff1, w_ff2, b_ff2,
             grouped = grouped_pool.tile([P, TILE_COLS, PACK], BF16, name="grouped", align_bytes=64)
             raw = raw_tiles[step]
             regroup(nc.vector.tensor_copy, grouped[:, 0:vector_cols, :], raw[:, :, 0:vector_cols])
-            regroup(nc.scalar.copy, grouped[:, vector_cols:TILE_COLS, :], raw[:, :, vector_cols:TILE_COLS])
+            scalar_to = TILE_COLS - tensor_cols(step)
+            if step in staged_banks:
+                nc.scalar.copy(out=grouped[:, scalar_to:TILE_COLS, :], in_=staged_banks[step][:])
+            if 0 <= step - 2 < FF1_STEPS:
+                gelu(step - 2)
+            regroup(nc.scalar.copy, grouped[:, vector_cols:scalar_to, :], raw[:, :, vector_cols:scalar_to])
             grouped_tiles[step] = grouped
+
+        def tensor_cols(step):
+            return TENSOR_COLS if 3 <= step < 2 + FF1_STEPS else 0
+
+        def regroup_on_tensor(step):
+            if tensor_cols(step) == 0:
+                return
+            staged_banks[step] = psum.tile([P, TENSOR_COLS, PACK], BF16, name="bank")
+            for c in range(0, TENSOR_COLS, UNIT):
+                first = TILE_COLS - TENSOR_COLS + c
+                nc.tensor.matmul(
+                    out=staged_banks[step][:, c : c + UNIT, :].rearrange("p c t -> p t c"),
+                    lhsT=ident_bf16[:],
+                    rhs=raw_tiles[step][:, :, first : first + UNIT],
+                    start=True,
+                    stop=True,
+                )
 
         def quantise_weights(step):
             operands = []
@@ -277,13 +302,12 @@ def tile_block_pa_kernel(tc, x, attn_merged, w_proj, w_ff1, b_ff1, w_ff2, b_ff2,
         for now in range(STEPS + 1):
             if now == ATTN_ROUND:
                 attn_grouped[0] = transpose_rows(attn_sb)
-            scalar_has_gelu = 0 <= now - 2 < FF1_STEPS
-            if scalar_has_gelu:
-                gelu(now - 2)
             if now == STEPS - 1:
                 multiply_into_result(now - 1, quantise_weights(now - 1))
             if now < STEPS:
                 regroup_weights(now, vector_cols(now))
+            if now + 1 < STEPS:
+                regroup_on_tensor(now + 1)
             if now == STEPS - 1:
                 for i in range(TOKEN_TILES - 1):
                     finish(0, i)

@@ -32,11 +32,11 @@ STEPS = FF1_STEPS + HALVES * HALF_STEPS
 RAW_BUFS = 8
 VECTOR_COLS_FIRST = 512
 VECTOR_COLS_BESIDE_GELU = 512
-VECTOR_COLS_ALONE = 480
+VECTOR_COLS_ALONE = 464
 VECTOR_COLS_LAST = 192
 TENSOR_COLS = 256
 UNIT = HALF // PACK
-ATTN_LOAD = 1
+ATTN_LOAD = 2
 ATTN_ROUND = 1
 
 FLOPS = 2 * TOKENS * (D * D + 2 * D * F)
@@ -63,9 +63,10 @@ def tile_block_pa_kernel(tc, x, attn_merged, w_proj, w_ff1, b_ff1, w_ff2, b_ff2,
         attn_sb = keep.tile([P, TOKEN_TILES, D], BF16, name="attn_sb")
         b2_row = keep.tile([P, D], BF16, name="b2_row")
         nc.gpsimd.memset(b2_row[:].bitcast(F32), 0.0)
-        nc.sync.dma_start(out=b2_row[0:1, :], in_=b_ff2.rearrange("(o d) -> o d", o=1))
         for i in range(TOKEN_TILES):
             nc.sync.dma_start(out=x_sb[:, i, :], in_=x_rows[i * P : (i + 1) * P, :])
+            if i == 0:
+                nc.sync.dma_start(out=b2_row[0:1, :], in_=b_ff2.rearrange("(o d) -> o d", o=1))
         ones = keep.tile([P, P], BF16, name="ones")
         nc.vector.memset(ones[:], 1.0)
         b1_rows = keep.tile([P, P], BF16, name="b1_rows")
@@ -206,7 +207,9 @@ def tile_block_pa_kernel(tc, x, attn_merged, w_proj, w_ff1, b_ff1, w_ff2, b_ff2,
                 nc.scalar.copy(out=grouped[:, scalar_to:TILE_COLS, :], in_=staged_banks[step][:])
             if 0 <= step - 2 < FF1_STEPS:
                 gelu(step - 2)
-            regroup(nc.scalar.copy, grouped[:, vector_cols:scalar_to, :], raw[:, :, vector_cols:scalar_to])
+            cuts = (vector_cols, HALF, TILE_COLS) if step == STEPS - 1 else (vector_cols, scalar_to)
+            for first, end in zip(cuts, cuts[1:]):
+                regroup(nc.scalar.copy, grouped[:, first:end, :], raw[:, :, first:end])
             grouped_tiles[step] = grouped
 
         def tensor_cols(step):
@@ -300,12 +303,12 @@ def tile_block_pa_kernel(tc, x, attn_merged, w_proj, w_ff1, b_ff1, w_ff2, b_ff2,
             return VECTOR_COLS_BESIDE_GELU if 0 <= step - 2 < FF1_STEPS else VECTOR_COLS_ALONE
 
         for now in range(STEPS + 1):
+            if now < STEPS:
+                regroup_weights(now, vector_cols(now))
             if now == ATTN_ROUND:
                 attn_grouped[0] = transpose_rows(attn_sb)
             if now == STEPS - 1:
                 multiply_into_result(now - 1, quantise_weights(now - 1))
-            if now < STEPS:
-                regroup_weights(now, vector_cols(now))
             if now + 1 < STEPS:
                 regroup_on_tensor(now + 1)
             if now == STEPS - 1:

@@ -30,12 +30,13 @@ HALF_STEPS = 1 + H_PASSES // TILE_PASSES
 HALVES = D // HALF
 STEPS = FF1_STEPS + HALVES * HALF_STEPS
 RAW_BUFS = 8
-VECTOR_COLS_FIRST = 512
-VECTOR_COLS_BESIDE_GELU = 512
+VECTOR_COLS_FIRST = 640
+VECTOR_COLS_BESIDE_GELU = 448
 VECTOR_COLS_ALONE = 464
 VECTOR_COLS_LAST = 192
-TENSOR_COLS = 256
+TENSOR_COLS = 384
 UNIT = HALF // PACK
+STAGED_COLS = 2 * UNIT
 ATTN_LOAD = 2
 ATTN_ROUND = 1
 
@@ -203,8 +204,8 @@ def tile_block_pa_kernel(tc, x, attn_merged, w_proj, w_ff1, b_ff1, w_ff2, b_ff2,
             raw = raw_tiles[step]
             regroup(nc.vector.tensor_copy, grouped[:, 0:vector_cols, :], raw[:, :, 0:vector_cols])
             scalar_to = TILE_COLS - tensor_cols(step)
-            if step in staged_banks:
-                nc.scalar.copy(out=grouped[:, scalar_to:TILE_COLS, :], in_=staged_banks[step][:])
+            for first, cols, bank in staged_banks.get(step, []):
+                nc.scalar.copy(out=grouped[:, first : first + cols, :], in_=bank[:, 0:cols, :])
             if 0 <= step - 2 < FF1_STEPS:
                 gelu(step - 2)
             cuts = (vector_cols, HALF, TILE_COLS) if step == STEPS - 1 else (vector_cols, scalar_to)
@@ -213,21 +214,22 @@ def tile_block_pa_kernel(tc, x, attn_merged, w_proj, w_ff1, b_ff1, w_ff2, b_ff2,
             grouped_tiles[step] = grouped
 
         def tensor_cols(step):
-            return TENSOR_COLS if 3 <= step < 2 + FF1_STEPS else 0
+            return TENSOR_COLS if 3 <= step <= 2 + FF1_STEPS else 0
 
         def regroup_on_tensor(step):
-            if tensor_cols(step) == 0:
-                return
-            staged_banks[step] = psum.tile([P, TENSOR_COLS, PACK], BF16, name="bank")
-            for c in range(0, TENSOR_COLS, UNIT):
-                first = TILE_COLS - TENSOR_COLS + c
-                nc.tensor.matmul(
-                    out=staged_banks[step][:, c : c + UNIT, :].rearrange("p c t -> p t c"),
-                    lhsT=ident_bf16[:],
-                    rhs=raw_tiles[step][:, :, first : first + UNIT],
-                    start=True,
-                    stop=True,
-                )
+            staged_banks[step] = []
+            for first in range(TILE_COLS - tensor_cols(step), TILE_COLS, STAGED_COLS):
+                cols = min(STAGED_COLS, TILE_COLS - first)
+                bank = psum.tile([P, STAGED_COLS, PACK], BF16, name="bank")
+                for c in range(0, cols, UNIT):
+                    nc.tensor.matmul(
+                        out=bank[:, c : c + UNIT, :].rearrange("p c t -> p t c"),
+                        lhsT=ident_bf16[:],
+                        rhs=raw_tiles[step][:, :, first + c : first + c + UNIT],
+                        start=True,
+                        stop=True,
+                    )
+                staged_banks[step].append((first, cols, bank))
 
         def quantise_weights(step):
             operands = []

@@ -37,6 +37,8 @@ VECTOR_COLS_LAST = 192
 TENSOR_COLS = 384
 UNIT = HALF // PACK
 STAGED_COLS = 2 * UNIT
+WARM_AHEAD = 7
+WARM_BEHIND = 2
 ATTN_LOAD = 2
 ATTN_ROUND = 1
 
@@ -157,6 +159,11 @@ def tile_block_pa_kernel(tc, x, attn_merged, w_proj, w_ff1, b_ff1, w_ff2, b_ff2,
                         in_=bank[:].rearrange("p u r -> p r u"),
                     )
             return grouped
+
+        def keep_tensor_busy(operands):
+            bank = psum.tile([P, HALF], F32, name="bank")
+            for rhs in operands:
+                nc.tensor.matmul(out=bank[:], lhsT=ident_bf16[:], rhs=rhs, start=True, stop=True)
 
         def quantise_rows(grouped, codes, scales):
             for g in range(D_PASSES):
@@ -308,7 +315,9 @@ def tile_block_pa_kernel(tc, x, attn_merged, w_proj, w_ff1, b_ff1, w_ff2, b_ff2,
             if now < STEPS:
                 regroup_weights(now, vector_cols(now))
             if now == ATTN_ROUND:
+                keep_tensor_busy([raw_tiles[now][:, n % PACK, 0:HALF] for n in range(WARM_AHEAD)])
                 attn_grouped[0] = transpose_rows(attn_sb)
+                keep_tensor_busy([attn_sb[:, n, 0:HALF] for n in range(WARM_BEHIND)])
             if now == STEPS - 1:
                 multiply_into_result(now - 1, quantise_weights(now - 1))
             if now + 1 < STEPS:

from contextlib import ExitStack

import concourse.mybir as mybir
from concourse.masks import make_identity

BF16 = mybir.dt.bfloat16
F32 = mybir.dt.float32
U32 = mybir.dt.uint32
U8 = mybir.dt.uint8
FP8X4 = mybir.dt.float8_e4m3fn_x4
GELU = mybir.ActivationFunctionType.Gelu
ADD = mybir.AluOpType.add

P = 128
PACK = 4
K_PASS = P * PACK
TOKENS = 512
TOKEN_TILES = TOKENS // P
D = 1024
F = 4096
HALF = 512
TILE_COLS = 2 * HALF
RUN = 8

D_PASSES = D // K_PASS
FF1_STEPS = F // HALF
H_PASSES = F // K_PASS
TILE_PASSES = TILE_COLS // HALF
HALF_STEPS = 1 + H_PASSES // TILE_PASSES
HALVES = D // HALF
STEPS = FF1_STEPS + HALVES * HALF_STEPS
RAW_BUFS = 8
VECTOR_COLS_FIRST = 640
VECTOR_COLS_BESIDE_GELU = 448
VECTOR_COLS_ALONE = 464
VECTOR_COLS_LAST = 192
TENSOR_COLS = 384
UNIT = HALF // PACK
STAGED_COLS = 2 * UNIT
WARM_AHEAD = 7
WARM_BEHIND = 2
ATTN_LOAD = 2
ATTN_ROUND = 1

FLOPS = 2 * TOKENS * (D * D + 2 * D * F)


def tile_block_pa_kernel(tc, x, attn_merged, w_proj, w_ff1, b_ff1, w_ff2, b_ff2, out):
    nc = tc.nc
    x_rows = x.flatten_outer_dims()
    attn_rows = attn_merged.flatten_outer_dims()
    out_rows = out.flatten_outer_dims()

    with ExitStack() as stack:
        stack.enter_context(tc.manual_schedule())
        keep = stack.enter_context(tc.tile_pool(name="keep", bufs=1))
        act_pool = stack.enter_context(tc.tile_pool(name="act", bufs=2))
        raw_pool = stack.enter_context(tc.tile_pool(name="raw", bufs=RAW_BUFS))
        grouped_pool = stack.enter_context(tc.tile_pool(name="grouped", bufs=3))
        codes_pool = stack.enter_context(tc.tile_pool(name="codes", bufs=3))
        h_pool = stack.enter_context(tc.tile_pool(name="h", bufs=2))
        out_pool = stack.enter_context(tc.tile_pool(name="result", bufs=4))
        psum = stack.enter_context(tc.psum_pool(name="psum", bufs=8))

        x_sb = keep.tile([P, TOKEN_TILES, D], BF16, name="x_sb")
        attn_sb = keep.tile([P, TOKEN_TILES, D], BF16, name="attn_sb")
        b2_row = keep.tile([P, D], BF16, name="b2_row")
        nc.gpsimd.memset(b2_row[:].bitcast(F32), 0.0)
        for i in range(TOKEN_TILES):
            nc.sync.dma_start(out=x_sb[:, i, :], in_=x_rows[i * P : (i + 1) * P, :])
            if i == 0:
                nc.sync.dma_start(out=b2_row[0:1, :], in_=b_ff2.rearrange("(o d) -> o d", o=1))
        ones = keep.tile([P, P], BF16, name="ones")
        nc.vector.memset(ones[:], 1.0)
        b1_rows = keep.tile([P, P], BF16, name="b1_rows")
        nc.vector.memset(b1_rows[:], 0.0)
        nc.scalar.dma_start(out=b1_rows[0 : F // P, :], in_=b_ff1.rearrange("(r c) -> r c", c=P))

        warm = keep.tile([P, 1], F32, name="warm")
        nc.vector.memset(warm[:], 0.0)
        nc.scalar.activation(out=warm[:], in_=warm[:], func=GELU)

        ident_f32 = keep.tile([P, P], F32, name="ident_f32")
        make_identity(nc, ident_f32[:])
        ident_bf16 = keep.tile([P, P], BF16, name="ident_bf16")
        make_identity(nc, ident_bf16[:])

        def load_weight_tile(step):
            raw = raw_pool.tile([P, PACK, TILE_COLS], BF16, name="raw")
            if step < FF1_STEPS:
                cols = slice(step * HALF, (step + 1) * HALF)
                for g in range(D_PASSES):
                    for u in range(2):
                        first = g * K_PASS + u * 2 * P
                        nc.sync.dma_start(
                            out=raw[:, 2 * u : 2 * u + 2, g * HALF : (g + 1) * HALF],
                            in_=w_ff1[first : first + 2 * P, cols].rearrange("(q e) c -> q e c", e=2),
                        )
            else:
                half, tile_of_half = divmod(step - FF1_STEPS, HALF_STEPS)
                cols = slice(half * HALF, (half + 1) * HALF)
                for g in range(TILE_PASSES):
                    to_cols = slice(g * HALF, (g + 1) * HALF)
                    if tile_of_half == 0:
                        for u in range(2):
                            first = g * K_PASS + u * 2 * P
                            nc.sync.dma_start(
                                out=raw[:, 2 * u : 2 * u + 2, to_cols],
                                in_=w_proj[first : first + 2 * P, cols].rearrange("(q e) n -> q e n", e=2),
                            )
                    else:
                        first = ((tile_of_half - 1) * TILE_PASSES + g) * K_PASS
                        nc.sync.dma_start(
                            out=raw[:, :, to_cols],
                            in_=w_ff2[first : first + K_PASS, cols].rearrange("(t p) n -> p t n", p=P),
                        )
            return raw

        def regroup(copy, grouped, rows):
            copy(
                out=grouped.rearrange("p (c i) t -> p c t i", i=RUN),
                in_=rows.rearrange("p t (c i) -> p c t i", i=RUN),
            )

        def quantise(grouped, codes, scales):
            nc.vector.quantize_mx(
                out=codes.bitcast(FP8X4),
                scales=scales,
                in_=grouped.rearrange("p c t -> p (c t)"),
            )

        raw_tiles = {}
        for step in range(RAW_BUFS):
            if step == ATTN_LOAD:
                for i in range(TOKEN_TILES):
                    nc.sync.dma_start(out=attn_sb[:, i, :], in_=attn_rows[i * P : (i + 1) * P, :])
            raw_tiles[step] = load_weight_tile(step)

        def x_words(rows_sb, i):
            return rows_sb[:, i, :].bitcast(F32)

        def transpose_rows(rows_sb):
            grouped = act_pool.tile([P, D_PASSES, TOKENS * PACK], BF16, name="act_grouped", align_bytes=64)
            for g in range(D_PASSES):
                grouped_words = grouped[:, g, :].bitcast(F32)
                for pair in range(TOKEN_TILES // 2):
                    bank = psum.tile([P, 2, 2 * P], F32, name="bank")
                    for u in range(2):
                        for j in range(2):
                            words = x_words(rows_sb, 2 * pair + j)
                            first = g * 2 * P + u * P
                            nc.tensor.transpose(
                                out=bank[:, u, j * P : (j + 1) * P],
                                in_=words[:, first : first + P],
                                identity=ident_f32[:],
                            )
                    nc.scalar.copy(
                        out=grouped_words[:, pair * 4 * P : (pair + 1) * 4 * P].rearrange("p (r u) -> p r u", u=2),
                        in_=bank[:].rearrange("p u r -> p r u"),
                    )
            return grouped

        def keep_tensor_busy(operands):
            bank = psum.tile([P, HALF], F32, name="bank")
            for rhs in operands:
                nc.tensor.matmul(out=bank[:], lhsT=ident_bf16[:], rhs=rhs, start=True, stop=True)

        def quantise_rows(grouped, codes, scales):
            for g in range(D_PASSES):
                nc.vector.quantize_mx(
                    out=codes[:, g, :].bitcast(FP8X4), scales=scales[:, g, :], in_=grouped[:, g, :]
                )

        x_codes = keep.tile([P, D_PASSES, TOKENS], U32, name="x_codes", align_bytes=64)
        x_scales = keep.tile([P, D_PASSES, TOKENS], U8, name="x_scales", align_bytes=64)
        attn_codes = keep.tile([P, D_PASSES, TOKENS], U32, name="attn_codes", align_bytes=64)
        attn_scales = keep.tile([P, D_PASSES, TOKENS], U8, name="attn_scales", align_bytes=64)

        x_plus_b2 = keep.tile([P, TOKEN_TILES, D], F32, name="x_plus_b2")
        b2_banks = []
        for half in range(2):
            b2_bank = psum.tile([P, HALF], F32, name="bank")
            nc.tensor.matmul(
                out=b2_bank[:], lhsT=ones[:], rhs=b2_row[:, half * HALF : (half + 1) * HALF], start=True, stop=True
            )
            b2_banks.append(b2_bank)
        for i in range(TOKEN_TILES):
            for half in range(2):
                cols = slice(half * HALF, (half + 1) * HALF)
                nc.vector.tensor_tensor(out=x_plus_b2[:, i, cols], in0=b2_banks[half][:], in1=x_sb[:, i, cols], op=ADD)

        quantise_rows(transpose_rows(x_sb), x_codes, x_scales)

        b1_bank = psum.tile([P, P], BF16, name="bank")
        nc.tensor.transpose(out=b1_bank[:], in_=b1_rows[:], identity=ident_bf16[:])
        b1 = keep.tile([P, F // P], F32, name="b1")
        nc.vector.tensor_copy(out=b1[:], in_=b1_bank[:, 0 : F // P])

        h_codes = keep.tile([P, H_PASSES, TOKENS], U32, name="h_codes", align_bytes=64)
        h_scales = keep.tile([P, H_PASSES, TOKENS], U8, name="h_scales", align_bytes=64)
        grouped_tiles = {}
        staged_banks = {}
        attn_grouped = {}
        hidden_banks = {}
        h_rows = {}
        h_grouped = {}
        acc = {}

        def regroup_weights(step, vector_cols):
            grouped = grouped_pool.tile([P, TILE_COLS, PACK], BF16, name="grouped", align_bytes=64)
            raw = raw_tiles[step]
            regroup(nc.vector.tensor_copy, grouped[:, 0:vector_cols, :], raw[:, :, 0:vector_cols])
            scalar_to = TILE_COLS - tensor_cols(step)
            for first, cols, bank in staged_banks.get(step, []):
                nc.scalar.copy(out=grouped[:, first : first + cols, :], in_=bank[:, 0:cols, :])
            if 0 <= step - 2 < FF1_STEPS:
                gelu(step - 2)
            cuts = (vector_cols, HALF, TILE_COLS) if step == STEPS - 1 else (vector_cols, scalar_to)
            for first, end in zip(cuts, cuts[1:]):
                regroup(nc.scalar.copy, grouped[:, first:end, :], raw[:, :, first:end])
            grouped_tiles[step] = grouped

        def tensor_cols(step):
            return TENSOR_COLS if 3 <= step <= 2 + FF1_STEPS else 0

        def regroup_on_tensor(step):
            staged_banks[step] = []
            for first in range(TILE_COLS - tensor_cols(step), TILE_COLS, STAGED_COLS):
                cols = min(STAGED_COLS, TILE_COLS - first)
                bank = psum.tile([P, STAGED_COLS, PACK], BF16, name="bank")
                for c in range(0, cols, UNIT):
                    nc.tensor.matmul(
                        out=bank[:, c : c + UNIT, :].rearrange("p c t -> p t c"),
                        lhsT=ident_bf16[:],
                        rhs=raw_tiles[step][:, :, first + c : first + c + UNIT],
                        start=True,
                        stop=True,
                    )
                staged_banks[step].append((first, cols, bank))

        def quantise_weights(step):
            operands = []
            for half in range(2):
                codes = codes_pool.tile([P, HALF], U32, name="codes%d" % half, align_bytes=64)
                scales = codes_pool.tile([P, HALF], U8, name="scales%d" % half, align_bytes=64)
                quantise(grouped_tiles[step][:, half * HALF : (half + 1) * HALF, :], codes[:], scales[:])
                operands.append((codes, scales))
            return operands

        def multiply_ff1(step, operands):
            hidden_banks[step] = []
            for t in range(PACK):
                bank = psum.tile([P, TOKENS], F32, name="bank")
                for g in range(D_PASSES):
                    codes, scales = operands[g]
                    nc.tensor.matmul_mx(
                        out=bank[:],
                        lhsT=codes[:, t * P : (t + 1) * P].bitcast(FP8X4),
                        lhsT_scale=scales[:, t * P : (t + 1) * P],
                        rhs=x_codes[:, g, :].bitcast(FP8X4),
                        rhs_scale=x_scales[:, g, :],
                        start=(g == 0),
                        stop=(g == D_PASSES - 1),
                    )
                hidden_banks[step].append(bank)

        def multiply_into_result(step, operands):
            half, tile_of_half = divmod(step - FF1_STEPS, HALF_STEPS)
            for g in range(TILE_PASSES):
                codes, scales = operands[g]
                if tile_of_half == 0:
                    k_pass, left_codes, left_scales = g, attn_codes, attn_scales
                else:
                    k_pass, left_codes, left_scales = (tile_of_half - 1) * TILE_PASSES + g, h_codes, h_scales
                opens = tile_of_half == 0 and g == 0
                for i in range(TOKEN_TILES):
                    if opens:
                        acc[(half, i)] = psum.tile([P, HALF], F32, name="bank")
                    nc.tensor.matmul_mx(
                        out=acc[(half, i)][:],
                        lhsT=left_codes[:, k_pass, i * P : (i + 1) * P].bitcast(FP8X4),
                        lhsT_scale=left_scales[:, k_pass, i * P : (i + 1) * P],
                        rhs=codes[:].bitcast(FP8X4),
                        rhs_scale=scales[:],
                        start=opens,
                        stop=(tile_of_half == HALF_STEPS - 1 and g == TILE_PASSES - 1),
                    )

        def finish(half, i):
            cols = slice(half * HALF, (half + 1) * HALF)
            result = out_pool.tile([P, HALF], F32, name="result")
            nc.vector.tensor_tensor(out=result[:], in0=acc[(half, i)][:], in1=x_plus_b2[:, i, cols], op=ADD)
            nc.sync.dma_start(out=out_rows[i * P : (i + 1) * P, cols], in_=result[:])

        def gelu(step):
            h_rows[step] = h_pool.tile([P, PACK, TOKENS], BF16, name="h_rows")
            for t in range(PACK):
                j = step * PACK + t
                nc.scalar.activation(
                    out=h_rows[step][:, t, :], in_=hidden_banks[step][t][:], func=GELU, bias=b1[:, j : j + 1]
                )

        def regroup_h(step):
            h_grouped[step] = h_pool.tile([P, TOKENS, PACK], BF16, name="h_grouped", align_bytes=64)
            regroup(nc.vector.tensor_copy, h_grouped[step][:], h_rows[step][:])

        def vector_cols(step):
            if step == 0:
                return VECTOR_COLS_FIRST
            if step == STEPS - 1:
                return VECTOR_COLS_LAST
            return VECTOR_COLS_BESIDE_GELU if 0 <= step - 2 < FF1_STEPS else VECTOR_COLS_ALONE

        for now in range(STEPS + 1):
            if now < STEPS:
                regroup_weights(now, vector_cols(now))
            if now == ATTN_ROUND:
                keep_tensor_busy([raw_tiles[now][:, n % PACK, 0:HALF] for n in range(WARM_AHEAD)])
                attn_grouped[0] = transpose_rows(attn_sb)
                keep_tensor_busy([attn_sb[:, n, 0:HALF] for n in range(WARM_BEHIND)])
            if now == STEPS - 1:
                multiply_into_result(now - 1, quantise_weights(now - 1))
            if now + 1 < STEPS:
                regroup_on_tensor(now + 1)
            if now == STEPS - 1:
                for i in range(TOKEN_TILES - 1):
                    finish(0, i)
            if now == ATTN_ROUND + 1:
                quantise_rows(attn_grouped[0], attn_codes, attn_scales)
            if 0 <= now - 4 < FF1_STEPS:
                quantise(h_grouped[now - 4][:], h_codes[:, now - 4, :], h_scales[:, now - 4, :])
            if 0 <= now - 3 < FF1_STEPS:
                regroup_h(now - 3)
            if 0 <= now - 1 and now != STEPS - 1:
                operands = quantise_weights(now - 1)
                if now - 1 < FF1_STEPS:
                    multiply_ff1(now - 1, operands)
                else:
                    multiply_into_result(now - 1, operands)
            if now + RAW_BUFS < STEPS:
                raw_tiles[now + RAW_BUFS] = load_weight_tile(now + RAW_BUFS)

        finish(0, TOKEN_TILES - 1)
        for i in range(TOKEN_TILES):
            finish(HALVES - 1, i)
